import numpy as np
import ml_dtypes


def mxq(x, axis, fmt="e4m3"):
    dtype, down = {"e4m3": (ml_dtypes.float8_e4m3fn, 7), "e5m2": (ml_dtypes.float8_e5m2, 14)}[fmt]
    v = np.moveaxis(np.asarray(x, np.float32).astype(ml_dtypes.bfloat16).astype(np.float64), axis, -1)
    blocks = v.reshape(v.shape[:-1] + (-1, 32))
    amax = np.abs(blocks).max(-1, keepdims=True)
    byte = np.maximum(np.where(amax > 0, np.frexp(amax)[1] - 1 + 127, 0) - down, 1)
    scale = np.exp2(byte - 127.0)
    codes = (blocks / scale).astype(np.float32).astype(dtype).astype(np.float64)
    return np.moveaxis((codes * scale).reshape(v.shape), -1, axis)


WIDE = False


def mx_kscale(k):
    if not WIDE:
        return np.ones(k)
    levels = np.array([10, -10, 5, -5, 0])
    if k % 512:
        return np.exp2(np.random.permutation(np.resize(levels, k // 32))).repeat(32)
    a = np.empty((k // 512, 16))
    for p in range(k // 512):
        a[p, :8] = np.random.permutation(np.resize(levels, 8))
        for g in range(8):
            far = levels[np.abs(levels - a[p, g]) >= 10]
            a[p, g + 8] = far[np.random.randint(len(far))]
    return np.exp2(a.ravel()).repeat(32)


BF16 = ml_dtypes.bfloat16


def bf(x):
    return np.asarray(x, np.float32).astype(BF16)


def f64(x):
    return np.asarray(x).astype(np.float64)


T, B, F, H, R, O = 1024, 8, 1024, 1024, 512, 128


def setup_inputs():
    s, t = mx_kscale(R), mx_kscale(H)
    return {"z2": bf(np.random.standard_normal((T, B, R)) * s),
            "sw1": bf(np.random.standard_normal((R, H)) / np.sqrt(R) / s[:, None] * t),
            "b2": bf(np.random.standard_normal((B, H)) * t),
            "w3": bf(np.random.standard_normal((B, H, O)) / np.sqrt(H) / t[:, None]),
            "b3": bf(np.random.standard_normal((B, O)))}


def reference(z2, sw1, b2, w3, b3):
    u = (mxq(f64(z2), 2, "e4m3").reshape(T * B, R) @ mxq(f64(sw1), 0, "e4m3")).reshape(T, B, H)
    h = np.maximum(u + f64(b2)[None, :, :], 0.0)
    out = (mxq(h, 2, "e4m3").transpose(1, 0, 2) @ mxq(f64(w3), 1, "e4m3")) + f64(b3)[:, None, :]
    return out.transpose(1, 0, 2)

@@ -1,0 +1,309 @@
+from contextlib import ExitStack
+
+import concourse.mybir as mybir
+from concourse.masks import make_identity
+
+F32 = mybir.dt.float32
+BF16 = mybir.dt.bfloat16
+U32 = mybir.dt.uint32
+U8 = mybir.dt.uint8
+FP8X4 = mybir.dt.float8_e4m3fn_x4
+RELU = mybir.ActivationFunctionType.Relu
+ADD = mybir.AluOpType.add
+
+T, B, R, H, O = 1024, 8, 512, 1024, 128
+P = 128
+PACK = 4
+UNIT = 512
+UNITS_PER_DATASET = T // UNIT
+UNITS = B * UNITS_PER_DATASET
+TOKEN_TILES = UNIT // P
+CHUNKS = H // P
+GROUPS = CHUNKS // PACK
+HALF = UNIT // 2
+PAIR = 2
+AHEAD = 4
+
+FLOPS = 2 * T * B * R * H + 2 * T * B * H * O
+
+
+def regroup(nc, grouped, planes):
+    nc.vector.tensor_copy(
+        out=grouped.rearrange("p (c i) t -> p c t i", i=4),
+        in_=planes.rearrange("p t (c i) -> p c t i", i=4),
+    )
+
+
+def quantise(nc, codes, scales, grouped):
+    nc.vector.quantize_mx(
+        out=codes.bitcast(FP8X4),
+        scales=scales,
+        in_=grouped.rearrange("p c t -> p (c t)"),
+    )
+
+
+def tile_mlpmodelpredictor_pb_t_kernel(tc, z2, sw1, b2, w3, b3, out):
+    nc = tc.nc
+    with ExitStack() as stack:
+        keep = stack.enter_context(tc.tile_pool(name="keep", bufs=1))
+        z_raw_pool = stack.enter_context(tc.tile_pool(name="z_raw", bufs=AHEAD))
+        w_pool = stack.enter_context(tc.tile_pool(name="w3", bufs=2))
+        z_pool = stack.enter_context(tc.tile_pool(name="z", bufs=2))
+        plane_pool = stack.enter_context(tc.tile_pool(name="planes", bufs=3))
+        h_pool = stack.enter_context(tc.tile_pool(name="h", bufs=2))
+        h_mx_pool = stack.enter_context(tc.tile_pool(name="h_mx", bufs=2 * GROUPS))
+        out_pool = stack.enter_context(tc.tile_pool(name="out", bufs=3))
+        psum_z = stack.enter_context(tc.psum_pool(name="psum_z", bufs=1))
+        psum_u = stack.enter_context(tc.psum_pool(name="psum_u", bufs=4))
+        psum_o = stack.enter_context(tc.psum_pool(name="psum_o", bufs=2))
+        stack.enter_context(tc.manual_schedule())
+
+        z_raw = {}
+        z_banks = {}
+        z_grouped = {}
+        z_mx = {}
+        planes = {}
+        h_grouped = {}
+        h_mx = {}
+        w_raw = {}
+        w_grouped = {}
+        w_mx = {}
+        o_banks = {}
+
+        def load_z(n):
+            b, s = divmod(n, UNITS_PER_DATASET)
+            rows = z_raw_pool.tile([P, TOKEN_TILES, R], BF16, name="z_rows")
+            nc.sync.dma_start(
+                out=rows[:],
+                in_=z2[s * UNIT : (s + 1) * UNIT, b, :].rearrange("(j p) r -> p j r", p=P),
+            )
+            z_raw[n] = rows
+
+        def load_s(col_half):
+            nc.sync.dma_start(
+                out=s_rows[:, col_half],
+                in_=sw1[:, col_half * UNIT : (col_half + 1) * UNIT].rearrange(
+                    "(p j) c -> p j c", j=PACK
+                ),
+            )
+
+        def load_w(b):
+            rows = w_pool.tile([P, GROUPS, PACK, O], BF16, name="w_rows")
+            nc.sync.dma_start(
+                out=rows[:], in_=w3[b].rearrange("(g p t) o -> p g t o", g=GROUPS, t=PACK)
+            )
+            w_raw[b] = rows
+
+        def transpose_z(n):
+            words = z_raw[n][:].bitcast(F32)
+            for half in range(UNIT // HALF):
+                bank = psum_z.tile([P, PAIR, HALF], F32, name="z_bank%d" % half)
+                for u in range(PAIR):
+                    for i in range(HALF // P):
+                        j = half * (HALF // P) + i
+                        nc.tensor.transpose(
+                            out=bank[:, u, i * P : (i + 1) * P],
+                            in_=words[:, j, u : PAIR * P : PAIR],
+                            identity=ident[:],
+                        )
+                z_banks[n, half] = bank
+
+        def copy_z(n, half, copy):
+            if half == 0:
+                z_grouped[n] = z_pool.tile([P, UNIT, PACK], BF16, name="z_grouped", align_bytes=64)
+            copy(
+                out=z_grouped[n][:].bitcast(F32)[:, half * HALF : (half + 1) * HALF, :],
+                in_=z_banks[n, half][:].rearrange("p u r -> p r u"),
+            )
+
+        def quantise_z(n):
+            codes = z_pool.tile([P, UNIT], U32, name="z_codes", align_bytes=64)
+            scales = z_pool.tile([P, UNIT], U8, name="z_scales", align_bytes=64)
+            quantise(nc, codes[:], scales[:], z_grouped[n][:])
+            z_mx[n] = (codes, scales)
+
+        def hidden(n, g):
+            b = n // UNITS_PER_DATASET
+            z_codes, z_scales = z_mx[n]
+            four = plane_pool.tile([P, PACK, UNIT], BF16, name="planes")
+            for t in range(PACK):
+                c = g * PACK + t
+                cols = slice(c * P, (c + 1) * P)
+                u_bank = psum_u.tile([P, UNIT], F32, name="u_bank")
+                nc.tensor.matmul_mx(
+                    out=u_bank[:],
+                    lhsT=s_codes[:, cols].bitcast(FP8X4),
+                    lhsT_scale=s_scales[:, cols],
+                    rhs=z_codes[:].bitcast(FP8X4),
+                    rhs_scale=z_scales[:],
+                    start=True,
+                    stop=True,
+                )
+                nc.scalar.activation(
+                    out=four[:, t, :],
+                    in_=u_bank[:],
+                    func=RELU,
+                    bias=b2_cols[:, t, b * GROUPS + g : b * GROUPS + g + 1],
+                    scale=1.0,
+                )
+            planes[n, g] = four
+
+        def regroup_h(n, g):
+            grouped = h_pool.tile([P, UNIT, PACK], BF16, name="h_grouped", align_bytes=64)
+            regroup(nc, grouped[:], planes[n, g][:])
+            h_grouped[n, g] = grouped
+
+        def quantise_h(n, g):
+            codes = h_mx_pool.tile([P, UNIT], U32, name="h_codes", align_bytes=64)
+            scales = h_mx_pool.tile([P, UNIT], U8, name="h_scales", align_bytes=64)
+            quantise(nc, codes[:], scales[:], h_grouped[n, g][:])
+            h_mx[n, g] = (codes, scales)
+
+        def regroup_w(b):
+            grouped = w_pool.tile([P, GROUPS * O, PACK], BF16, name="w_grouped", align_bytes=64)
+            for g in range(GROUPS):
+                regroup(
+                    nc,
+                    grouped[:, g * O : (g + 1) * O, :],
+                    w_raw[b][:, g],
+                )
+            w_grouped[b] = grouped
+
+        def quantise_w(b):
+            codes = w_pool.tile([P, GROUPS * O], U32, name="w_codes", align_bytes=64)
+            scales = w_pool.tile([P, GROUPS * O], U8, name="w_scales", align_bytes=64)
+            quantise(nc, codes[:], scales[:], w_grouped[b][:])
+            w_mx[b] = (codes, scales)
+
+        def output(n):
+            w_codes, w_scales = w_mx[n // UNITS_PER_DATASET]
+            o_bank = psum_o.tile([P, TOKEN_TILES, O], F32, name="o_bank")
+            for j in range(TOKEN_TILES):
+                tokens = slice(j * P, (j + 1) * P)
+                for g in range(GROUPS):
+                    h_codes, h_scales = h_mx[n, g]
+                    w_cols = slice(g * O, (g + 1) * O)
+                    nc.tensor.matmul_mx(
+                        out=o_bank[:, j, :],
+                        lhsT=h_codes[:, tokens].bitcast(FP8X4),
+                        lhsT_scale=h_scales[:, tokens],
+                        rhs=w_codes[:, w_cols].bitcast(FP8X4),
+                        rhs_scale=w_scales[:, w_cols],
+                        start=(g == 0),
+                        stop=(g == GROUPS - 1),
+                    )
+            o_banks[n] = o_bank
+
+        def store(n):
+            b, s = divmod(n, UNITS_PER_DATASET)
+            result = out_pool.tile([P, TOKEN_TILES, O], F32, name="result")
+            nc.vector.tensor_tensor(
+                out=result[:],
+                in0=o_banks[n][:],
+                in1=b3_all[:, b, :].unsqueeze(1).to_broadcast([P, TOKEN_TILES, O]),
+                op=ADD,
+            )
+            nc.sync.dma_start(
+                out=out[s * UNIT : (s + 1) * UNIT, b, :].rearrange("(j p) o -> p j o", p=P),
+                in_=result[:],
+            )
+
+        s_rows = keep.tile([P, 2, PACK, UNIT], BF16, name="s_rows")
+        b2_rows = keep.tile([P, P * PACK], BF16, name="b2_rows")
+        b3_all = keep.tile([P, B, O], BF16, name="b3_all")
+        nc.vector.memset(b2_rows[:], 0.0)
+        nc.sync.dma_start(
+            out=b2_rows[0 : B * GROUPS, :], in_=b2.rearrange("b (g c) -> (b g) c", g=GROUPS)
+        )
+        load_s(0)
+        load_z(0)
+        load_z(1)
+        load_s(1)
+        load_z(2)
+        load_w(0)
+        load_z(3)
+        nc.sync.dma_start(
+            out=b3_all[:].rearrange("p b o -> p (b o)"),
+            in_=b3.rearrange("b o -> (b o)").partition_broadcast(P),
+        )
+
+        ident = keep.tile([P, P], F32, name="ident")
+        make_identity(nc, ident[:])
+
+        b2_rows_f32 = keep.tile([P, PACK, P], F32, name="b2_rows_f32")
+        nc.vector.tensor_copy(
+            out=b2_rows_f32[:], in_=b2_rows[:].rearrange("q (p t) -> q t p", t=PACK)
+        )
+        b2_bank = psum_o.tile([P, TOKEN_TILES, O], F32, name="o_bank")
+        for t in range(PACK):
+            nc.tensor.transpose(out=b2_bank[:, t, :], in_=b2_rows_f32[:, t, :], identity=ident[:])
+        b2_cols = keep.tile([P, PACK, B * GROUPS], F32, name="b2_cols")
+        nc.vector.tensor_copy(out=b2_cols[:], in_=b2_bank[:, :, 0 : B * GROUPS])
+
+        s_grouped = keep.tile([P, 2, UNIT, PACK], BF16, name="s_grouped", align_bytes=64)
+        s_codes = keep.tile([P, H], U32, name="s_codes", align_bytes=64)
+        s_scales = keep.tile([P, H], U8, name="s_scales", align_bytes=64)
+
+        def regroup_s(col_half):
+            for t in range(PACK):
+                nc.vector.tensor_copy(
+                    out=s_grouped[:, col_half, t * P : (t + 1) * P, :].rearrange(
+                        "p (m i) j -> p m j i", i=2
+                    ),
+                    in_=s_rows[:, col_half].rearrange("p j (m i t) -> p t m j i", i=2, t=PACK)[
+                        :, t
+                    ],
+                )
+
+        def quantise_s(col_half):
+            cols = slice(col_half * UNIT, (col_half + 1) * UNIT)
+            quantise(nc, s_codes[:, cols], s_scales[:, cols], s_grouped[:, col_half])
+
+        regroup_s(0)
+        transpose_z(0)
+        quantise_s(0)
+        copy_z(0, 0, nc.scalar.copy)
+        copy_z(0, 1, nc.vector.tensor_copy)
+        quantise_z(0)
+        transpose_z(1)
+        regroup_s(1)
+        copy_z(1, 0, nc.vector.tensor_copy)
+        quantise_s(1)
+        copy_z(1, 1, nc.vector.tensor_copy)
+
+        def live(n):
+            return 0 <= n < UNITS
+
+        for n in range(UNITS + 2):
+            b = n // UNITS_PER_DATASET
+            new_dataset = live(n) and n % UNITS_PER_DATASET == 0
+            if live(n + AHEAD):
+                load_z(n + AHEAD)
+            if new_dataset and b + 1 < B:
+                load_w(b + 1)
+            if live(n - 1):
+                regroup_h(n - 1, 1)
+            if live(n + 1):
+                quantise_z(n + 1)
+            if live(n):
+                hidden(n, 0)
+            if live(n - 1):
+                quantise_h(n - 1, 1)
+            if live(n + 2):
+                transpose_z(n + 2)
+                copy_z(n + 2, 0, nc.scalar.copy)
+                copy_z(n + 2, 1, nc.scalar.copy if new_dataset else nc.vector.tensor_copy)
+            if live(n):
+                hidden(n, 1)
+            if live(n - 1):
+                output(n - 1)
+            if live(n):
+                regroup_h(n, 0)
+            if new_dataset:
+                regroup_w(b)
+            if live(n - 2):
+                store(n - 2)
+            if live(n):
+                quantise_h(n, 0)
+            if new_dataset:
+                quantise_w(b)

@@ -23,12 +23,14 @@ GROUPS = CHUNKS // PACK
 HALF = UNIT // 2
 PAIR = 2
 AHEAD = 4
+HALVES = [(0, HALF), (HALF, UNIT)]
+LAST_PIECES = [(0, HALF), (HALF, HALF + P), (HALF + P, UNIT)]
 
 FLOPS = 2 * T * B * R * H + 2 * T * B * H * O
 
 
-def regroup(nc, grouped, planes):
-    nc.vector.tensor_copy(
+def regroup(copy, grouped, planes):
+    copy(
         out=grouped.rearrange("p (c i) t -> p c t i", i=4),
         in_=planes.rearrange("p t (c i) -> p c t i", i=4),
     )
@@ -49,7 +51,7 @@ def tile_mlpmodelpredictor_pb_t_kernel(tc, z2, sw1, b2, w3, b3, out):
         z_raw_pool = stack.enter_context(tc.tile_pool(name="z_raw", bufs=AHEAD))
         w_pool = stack.enter_context(tc.tile_pool(name="w3", bufs=2))
         z_pool = stack.enter_context(tc.tile_pool(name="z", bufs=2))
-        plane_pool = stack.enter_context(tc.tile_pool(name="planes", bufs=3))
+        plane_pool = stack.enter_context(tc.tile_pool(name="planes", bufs=4))
         h_pool = stack.enter_context(tc.tile_pool(name="h", bufs=2))
         h_mx_pool = stack.enter_context(tc.tile_pool(name="h_mx", bufs=2 * GROUPS))
         out_pool = stack.enter_context(tc.tile_pool(name="out", bufs=3))
@@ -70,14 +72,14 @@ def tile_mlpmodelpredictor_pb_t_kernel(tc, z2, sw1, b2, w3, b3, out):
         w_mx = {}
         o_banks = {}
 
-        def load_z(n):
+        def load_z(n, lo=0, hi=UNIT):
             b, s = divmod(n, UNITS_PER_DATASET)
-            rows = z_raw_pool.tile([P, TOKEN_TILES, R], BF16, name="z_rows")
+            if lo == 0:
+                z_raw[n] = z_raw_pool.tile([P, TOKEN_TILES, R], BF16, name="z_rows")
             nc.sync.dma_start(
-                out=rows[:],
-                in_=z2[s * UNIT : (s + 1) * UNIT, b, :].rearrange("(j p) r -> p j r", p=P),
+                out=z_raw[n][:, lo // P : hi // P, :],
+                in_=z2[s * UNIT + lo : s * UNIT + hi, b, :].rearrange("(j p) r -> p j r", p=P),
             )
-            z_raw[n] = rows
 
         def load_s(col_half):
             nc.sync.dma_start(
@@ -94,19 +96,17 @@ def tile_mlpmodelpredictor_pb_t_kernel(tc, z2, sw1, b2, w3, b3, out):
             )
             w_raw[b] = rows
 
-        def transpose_z(n):
+        def transpose_z(n, half):
             words = z_raw[n][:].bitcast(F32)
-            for half in range(UNIT // HALF):
-                bank = psum_z.tile([P, PAIR, HALF], F32, name="z_bank%d" % half)
+            bank = psum_z.tile([P, PAIR, HALF], F32, name="z_bank%d" % half)
+            for i in range(HALF // P):
                 for u in range(PAIR):
-                    for i in range(HALF // P):
-                        j = half * (HALF // P) + i
-                        nc.tensor.transpose(
-                            out=bank[:, u, i * P : (i + 1) * P],
-                            in_=words[:, j, u : PAIR * P : PAIR],
-                            identity=ident[:],
-                        )
-                z_banks[n, half] = bank
+                    nc.tensor.transpose(
+                        out=bank[:, u, i * P : (i + 1) * P],
+                        in_=words[:, half * (HALF // P) + i, u : PAIR * P : PAIR],
+                        identity=ident[:],
+                    )
+            z_banks[n, half] = bank
 
         def copy_z(n, half, copy):
             if half == 0:
@@ -116,54 +116,63 @@ def tile_mlpmodelpredictor_pb_t_kernel(tc, z2, sw1, b2, w3, b3, out):
                 in_=z_banks[n, half][:].rearrange("p u r -> p r u"),
             )
 
-        def quantise_z(n):
-            codes = z_pool.tile([P, UNIT], U32, name="z_codes", align_bytes=64)
-            scales = z_pool.tile([P, UNIT], U8, name="z_scales", align_bytes=64)
-            quantise(nc, codes[:], scales[:], z_grouped[n][:])
-            z_mx[n] = (codes, scales)
+        def quantise_z(n, lo=0, hi=UNIT):
+            if lo == 0:
+                codes = z_pool.tile([P, UNIT], U32, name="z_codes", align_bytes=64)
+                scales = z_pool.tile([P, UNIT], U8, name="z_scales", align_bytes=64)
+                z_mx[n] = (codes, scales)
+            codes, scales = z_mx[n]
+            quantise(nc, codes[:, lo:hi], scales[:, lo:hi], z_grouped[n][:, lo:hi])
 
-        def hidden(n, g):
+        def hidden_chunk(n, g, t, lo=0, hi=UNIT):
             b = n // UNITS_PER_DATASET
             z_codes, z_scales = z_mx[n]
-            four = plane_pool.tile([P, PACK, UNIT], BF16, name="planes")
+            if lo == 0 and t == 0:
+                planes[n, g] = plane_pool.tile([P, PACK, UNIT], BF16, name="planes")
+            c = g * PACK + t
+            cols = slice(c * P, (c + 1) * P)
+            u_bank = psum_u.tile([P, UNIT], F32, name="u_bank")
+            nc.tensor.matmul_mx(
+                out=u_bank[:, 0 : hi - lo],
+                lhsT=s_codes[:, cols].bitcast(FP8X4),
+                lhsT_scale=s_scales[:, cols],
+                rhs=z_codes[:, lo:hi].bitcast(FP8X4),
+                rhs_scale=z_scales[:, lo:hi],
+                start=True,
+                stop=True,
+            )
+            nc.scalar.activation(
+                out=planes[n, g][:, t, lo:hi],
+                in_=u_bank[:, 0 : hi - lo],
+                func=RELU,
+                bias=b2_cols[:, t, b * GROUPS + g : b * GROUPS + g + 1],
+                scale=1.0,
+            )
+
+        def hidden(n, g, lo=0, hi=UNIT):
             for t in range(PACK):
-                c = g * PACK + t
-                cols = slice(c * P, (c + 1) * P)
-                u_bank = psum_u.tile([P, UNIT], F32, name="u_bank")
-                nc.tensor.matmul_mx(
-                    out=u_bank[:],
-                    lhsT=s_codes[:, cols].bitcast(FP8X4),
-                    lhsT_scale=s_scales[:, cols],
-                    rhs=z_codes[:].bitcast(FP8X4),
-                    rhs_scale=z_scales[:],
-                    start=True,
-                    stop=True,
+                hidden_chunk(n, g, t, lo, hi)
+
+        def regroup_h(n, g, lo=0, hi=UNIT):
+            if lo == 0:
+                h_grouped[n, g] = h_pool.tile(
+                    [P, UNIT, PACK], BF16, name="h_grouped", align_bytes=64
                 )
-                nc.scalar.activation(
-                    out=four[:, t, :],
-                    in_=u_bank[:],
-                    func=RELU,
-                    bias=b2_cols[:, t, b * GROUPS + g : b * GROUPS + g + 1],
-                    scale=1.0,
-                )
-            planes[n, g] = four
+            regroup(nc.vector.tensor_copy, h_grouped[n, g][:, lo:hi], planes[n, g][:, :, lo:hi])
 
-        def regroup_h(n, g):
-            grouped = h_pool.tile([P, UNIT, PACK], BF16, name="h_grouped", align_bytes=64)
-            regroup(nc, grouped[:], planes[n, g][:])
-            h_grouped[n, g] = grouped
+        def quantise_h(n, g, lo=0, hi=UNIT):
+            if lo == 0:
+                codes = h_mx_pool.tile([P, UNIT], U32, name="h_codes", align_bytes=64)
+                scales = h_mx_pool.tile([P, UNIT], U8, name="h_scales", align_bytes=64)
+                h_mx[n, g] = (codes, scales)
+            codes, scales = h_mx[n, g]
+            quantise(nc, codes[:, lo:hi], scales[:, lo:hi], h_grouped[n, g][:, lo:hi])
 
-        def quantise_h(n, g):
-            codes = h_mx_pool.tile([P, UNIT], U32, name="h_codes", align_bytes=64)
-            scales = h_mx_pool.tile([P, UNIT], U8, name="h_scales", align_bytes=64)
-            quantise(nc, codes[:], scales[:], h_grouped[n, g][:])
-            h_mx[n, g] = (codes, scales)
-
-        def regroup_w(b):
+        def regroup_w(b, copy):
             grouped = w_pool.tile([P, GROUPS * O, PACK], BF16, name="w_grouped", align_bytes=64)
             for g in range(GROUPS):
                 regroup(
-                    nc,
+                    copy,
                     grouped[:, g * O : (g + 1) * O, :],
                     w_raw[b][:, g],
                 )
@@ -175,10 +184,10 @@ def tile_mlpmodelpredictor_pb_t_kernel(tc, z2, sw1, b2, w3, b3, out):
             quantise(nc, codes[:], scales[:], w_grouped[b][:])
             w_mx[b] = (codes, scales)
 
-        def output(n):
+        def output(n, lo=0, hi=UNIT):
             w_codes, w_scales = w_mx[n // UNITS_PER_DATASET]
             o_bank = psum_o.tile([P, TOKEN_TILES, O], F32, name="o_bank")
-            for j in range(TOKEN_TILES):
+            for j in range(lo // P, hi // P):
                 tokens = slice(j * P, (j + 1) * P)
                 for g in range(GROUPS):
                     h_codes, h_scales = h_mx[n, g]
@@ -192,33 +201,35 @@ def tile_mlpmodelpredictor_pb_t_kernel(tc, z2, sw1, b2, w3, b3, out):
                         start=(g == 0),
                         stop=(g == GROUPS - 1),
                     )
-            o_banks[n] = o_bank
+            o_banks[n, lo] = o_bank
 
-        def store(n):
+        def store(n, lo=0, hi=UNIT):
             b, s = divmod(n, UNITS_PER_DATASET)
+            tiles = slice(lo // P, hi // P)
             result = out_pool.tile([P, TOKEN_TILES, O], F32, name="result")
             nc.vector.tensor_tensor(
-                out=result[:],
-                in0=o_banks[n][:],
-                in1=b3_all[:, b, :].unsqueeze(1).to_broadcast([P, TOKEN_TILES, O]),
+                out=result[:, tiles, :],
+                in0=o_banks[n, lo][:, tiles, :],
+                in1=b3_all[:, b, :].unsqueeze(1).to_broadcast([P, (hi - lo) // P, O]),
                 op=ADD,
             )
             nc.sync.dma_start(
-                out=out[s * UNIT : (s + 1) * UNIT, b, :].rearrange("(j p) o -> p j o", p=P),
-                in_=result[:],
+                out=out[s * UNIT + lo : s * UNIT + hi, b, :].rearrange("(j p) o -> p j o", p=P),
+                in_=result[:, tiles, :],
             )
 
         s_rows = keep.tile([P, 2, PACK, UNIT], BF16, name="s_rows")
         b2_rows = keep.tile([P, P * PACK], BF16, name="b2_rows")
         b3_all = keep.tile([P, B, O], BF16, name="b3_all")
         nc.vector.memset(b2_rows[:], 0.0)
+        load_z(0, 0, HALF)
         nc.sync.dma_start(
             out=b2_rows[0 : B * GROUPS, :], in_=b2.rearrange("b (g c) -> (b g) c", g=GROUPS)
         )
         load_s(0)
-        load_z(0)
-        load_z(1)
+        load_z(0, HALF, UNIT)
         load_s(1)
+        load_z(1)
         load_z(2)
         load_w(0)
         load_z(3)
@@ -231,79 +242,115 @@ def tile_mlpmodelpredictor_pb_t_kernel(tc, z2, sw1, b2, w3, b3, out):
         make_identity(nc, ident[:])
 
         b2_rows_f32 = keep.tile([P, PACK, P], F32, name="b2_rows_f32")
+        b2_cols = keep.tile([P, PACK, B * GROUPS], F32, name="b2_cols")
+        s_grouped = keep.tile([P, 2, UNIT, PACK], BF16, name="s_grouped", align_bytes=64)
+        s_codes = keep.tile([P, H], U32, name="s_codes", align_bytes=64)
+        s_scales = keep.tile([P, H], U8, name="s_scales", align_bytes=64)
+
+        def regroup_s(col_half, t, copy):
+            copy(
+                out=s_grouped[:, col_half, t * P : (t + 1) * P, :].rearrange(
+                    "p (m i) j -> p m j i", i=2
+                ),
+                in_=s_rows[:, col_half].rearrange("p j (m i t) -> p t m j i", i=2, t=PACK)[:, t],
+            )
+
+        def quantise_s(col_half, t0, t1):
+            cols = slice(col_half * UNIT + t0 * P, col_half * UNIT + t1 * P)
+            quantise(
+                nc, s_codes[:, cols], s_scales[:, cols], s_grouped[:, col_half, t0 * P : t1 * P]
+            )
+
+        transpose_z(0, 0)
+        copy_z(0, 0, nc.scalar.copy)
         nc.vector.tensor_copy(
             out=b2_rows_f32[:], in_=b2_rows[:].rearrange("q (p t) -> q t p", t=PACK)
         )
         b2_bank = psum_o.tile([P, TOKEN_TILES, O], F32, name="o_bank")
         for t in range(PACK):
             nc.tensor.transpose(out=b2_bank[:, t, :], in_=b2_rows_f32[:, t, :], identity=ident[:])
-        b2_cols = keep.tile([P, PACK, B * GROUPS], F32, name="b2_cols")
+        transpose_z(0, 1)
+        regroup_s(0, 0, nc.vector.tensor_copy)
+        regroup_s(0, 1, nc.scalar.copy)
+        quantise_z(0, 0, HALF)
+        quantise_s(0, 0, 1)
         nc.vector.tensor_copy(out=b2_cols[:], in_=b2_bank[:, :, 0 : B * GROUPS])
+        copy_z(0, 1, nc.scalar.copy)
+        hidden_chunk(0, 0, 0, 0, HALF)
+        regroup_s(0, 2, nc.vector.tensor_copy)
+        quantise_s(0, 1, 2)
+        hidden_chunk(0, 0, 1, 0, HALF)
+        regroup_s(0, 3, nc.vector.tensor_copy)
+        quantise_s(0, 2, 3)
+        hidden_chunk(0, 0, 2, 0, HALF)
+        quantise_s(0, 3, 4)
+        hidden_chunk(0, 0, 3, 0, HALF)
+        quantise_z(0, HALF, UNIT)
+        hidden(0, 0, HALF, UNIT)
+        transpose_z(1, 0)
+        transpose_z(1, 1)
+        for t in range(PACK):
+            regroup_s(1, t, nc.vector.tensor_copy)
+        quantise_s(1, 0, PACK)
+        copy_z(1, 0, nc.scalar.copy)
+        copy_z(1, 1, nc.scalar.copy)
+        hidden(0, 1)
+        regroup_h(0, 0)
+        quantise_z(1)
+        quantise_h(0, 0)
+        load_z(4)
+        load_w(1)
+        regroup_w(0, nc.vector.tensor_copy)
+        transpose_z(2, 0)
+        transpose_z(2, 1)
+        copy_z(2, 0, nc.scalar.copy)
+        copy_z(2, 1, nc.scalar.copy)
+        quantise_w(0)
 
-        s_grouped = keep.tile([P, 2, UNIT, PACK], BF16, name="s_grouped", align_bytes=64)
-        s_codes = keep.tile([P, H], U32, name="s_codes", align_bytes=64)
-        s_scales = keep.tile([P, H], U8, name="s_scales", align_bytes=64)
-
-        def regroup_s(col_half):
-            for t in range(PACK):
-                nc.vector.tensor_copy(
-                    out=s_grouped[:, col_half, t * P : (t + 1) * P, :].rearrange(
-                        "p (m i) j -> p m j i", i=2
-                    ),
-                    in_=s_rows[:, col_half].rearrange("p j (m i t) -> p t m j i", i=2, t=PACK)[
-                        :, t
-                    ],
-                )
-
-        def quantise_s(col_half):
-            cols = slice(col_half * UNIT, (col_half + 1) * UNIT)
-            quantise(nc, s_codes[:, cols], s_scales[:, cols], s_grouped[:, col_half])
-
-        regroup_s(0)
-        transpose_z(0)
-        quantise_s(0)
-        copy_z(0, 0, nc.scalar.copy)
-        copy_z(0, 1, nc.vector.tensor_copy)
-        quantise_z(0)
-        transpose_z(1)
-        regroup_s(1)
-        copy_z(1, 0, nc.vector.tensor_copy)
-        quantise_s(1)
-        copy_z(1, 1, nc.vector.tensor_copy)
-
-        def live(n):
-            return 0 <= n < UNITS
-
-        for n in range(UNITS + 2):
+        last = UNITS - 1
+        for n in range(1, last):
             b = n // UNITS_PER_DATASET
-            new_dataset = live(n) and n % UNITS_PER_DATASET == 0
-            if live(n + AHEAD):
+            new_dataset = n % UNITS_PER_DATASET == 0
+            if n + AHEAD < UNITS:
                 load_z(n + AHEAD)
             if new_dataset and b + 1 < B:
                 load_w(b + 1)
-            if live(n - 1):
-                regroup_h(n - 1, 1)
-            if live(n + 1):
-                quantise_z(n + 1)
-            if live(n):
-                hidden(n, 0)
-            if live(n - 1):
-                quantise_h(n - 1, 1)
-            if live(n + 2):
-                transpose_z(n + 2)
+            regroup_h(n - 1, 1)
+            quantise_z(n + 1)
+            hidden(n, 0)
+            quantise_h(n - 1, 1)
+            if n + 2 < UNITS:
+                transpose_z(n + 2, 0)
+                transpose_z(n + 2, 1)
                 copy_z(n + 2, 0, nc.scalar.copy)
                 copy_z(n + 2, 1, nc.scalar.copy if new_dataset else nc.vector.tensor_copy)
-            if live(n):
-                hidden(n, 1)
-            if live(n - 1):
-                output(n - 1)
-            if live(n):
-                regroup_h(n, 0)
-            if new_dataset:
-                regroup_w(b)
-            if live(n - 2):
-                store(n - 2)
-            if live(n):
-                quantise_h(n, 0)
+            elif new_dataset:
+                regroup_w(b, nc.scalar.copy)
+            for lo, hi in HALVES if n + 1 == last else [(0, UNIT)]:
+                hidden(n, 1, lo, hi)
+            output(n - 1)
+            regroup_h(n, 0)
+            if new_dataset and n + 2 < UNITS:
+                regroup_w(b, nc.vector.tensor_copy)
+            store(n - 1)
             if new_dataset:
                 quantise_w(b)
+            quantise_h(n, 0)
+
+        for lo, hi in HALVES:
+            regroup_h(last - 1, 1, lo, hi)
+        for lo, hi in HALVES:
+            quantise_h(last - 1, 1, lo, hi)
+        before = (last - 1, 0, UNIT)
+        for lo, hi in LAST_PIECES:
+            for g in range(GROUPS):
+                hidden(last, g, lo, hi)
+            output(*before)
+            for g in range(GROUPS):
+                regroup_h(last, g, lo, hi)
+            store(*before)
+            for g in range(GROUPS):
+                quantise_h(last, g, lo, hi)
+            before = (last, lo, hi)
+        output(*before)
+        store(*before)

@@ -53,7 +53,7 @@ def tile_mlpmodelpredictor_pb_t_kernel(tc, z2, sw1, b2, w3, b3, out):
         z_pool = stack.enter_context(tc.tile_pool(name="z", bufs=2))
         plane_pool = stack.enter_context(tc.tile_pool(name="planes", bufs=4))
         h_pool = stack.enter_context(tc.tile_pool(name="h", bufs=2))
-        h_mx_pool = stack.enter_context(tc.tile_pool(name="h_mx", bufs=2 * GROUPS))
+        h_mx_pool = stack.enter_context(tc.tile_pool(name="h_mx", bufs=3 * GROUPS))
         out_pool = stack.enter_context(tc.tile_pool(name="out", bufs=3))
         psum_z = stack.enter_context(tc.psum_pool(name="psum_z", bufs=1))
         psum_u = stack.enter_context(tc.psum_pool(name="psum_u", bufs=4))
@@ -318,25 +318,27 @@ def tile_mlpmodelpredictor_pb_t_kernel(tc, z2, sw1, b2, w3, b3, out):
             regroup_h(n - 1, 1)
             quantise_z(n + 1)
             hidden(n, 0)
+            if n >= 2:
+                output(n - 2)
             quantise_h(n - 1, 1)
             if n + 2 < UNITS:
                 transpose_z(n + 2, 0)
                 transpose_z(n + 2, 1)
                 copy_z(n + 2, 0, nc.scalar.copy)
                 copy_z(n + 2, 1, nc.scalar.copy if new_dataset else nc.vector.tensor_copy)
-            elif new_dataset:
-                regroup_w(b, nc.scalar.copy)
             for lo, hi in HALVES if n + 1 == last else [(0, UNIT)]:
                 hidden(n, 1, lo, hi)
-            output(n - 1)
             regroup_h(n, 0)
-            if new_dataset and n + 2 < UNITS:
+            if new_dataset:
                 regroup_w(b, nc.vector.tensor_copy)
-            store(n - 1)
+            if n >= 2:
+                store(n - 2)
             if new_dataset:
                 quantise_w(b)
             quantise_h(n, 0)
 
+        output(last - 2)
+        store(last - 2)
         for lo, hi in HALVES:
             regroup_h(last - 1, 1, lo, hi)
         for lo, hi in HALVES:

@@ -10,6 +10,7 @@ U8 = mybir.dt.uint8
 FP8X4 = mybir.dt.float8_e4m3fn_x4
 RELU = mybir.ActivationFunctionType.Relu
 ADD = mybir.AluOpType.add
+MULT = mybir.AluOpType.mult
 
 T, B, R, H, O = 1024, 8, 512, 1024, 128
 P = 128
@@ -153,12 +154,12 @@ def tile_mlpmodelpredictor_pb_t_kernel(tc, z2, sw1, b2, w3, b3, out):
             for t in range(PACK):
                 hidden_chunk(n, g, t, lo, hi)
 
-        def regroup_h(n, g, lo=0, hi=UNIT):
+        def regroup_h(n, g, lo=0, hi=UNIT, copy=nc.vector.tensor_copy):
             if lo == 0:
                 h_grouped[n, g] = h_pool.tile(
                     [P, UNIT, PACK], BF16, name="h_grouped", align_bytes=64
                 )
-            regroup(nc.vector.tensor_copy, h_grouped[n, g][:, lo:hi], planes[n, g][:, :, lo:hi])
+            regroup(copy, h_grouped[n, g][:, lo:hi], planes[n, g][:, :, lo:hi])
 
         def quantise_h(n, g, lo=0, hi=UNIT):
             if lo == 0:
@@ -168,21 +169,28 @@ def tile_mlpmodelpredictor_pb_t_kernel(tc, z2, sw1, b2, w3, b3, out):
             codes, scales = h_mx[n, g]
             quantise(nc, codes[:, lo:hi], scales[:, lo:hi], h_grouped[n, g][:, lo:hi])
 
-        def regroup_w(b, copy):
-            grouped = w_pool.tile([P, GROUPS * O, PACK], BF16, name="w_grouped", align_bytes=64)
-            for g in range(GROUPS):
-                regroup(
-                    copy,
-                    grouped[:, g * O : (g + 1) * O, :],
-                    w_raw[b][:, g],
-                )
-            w_grouped[b] = grouped
+        def regroup_w(m):
+            b, g = divmod(m, GROUPS)
+            grouped = keep.tile([P, O, PACK], BF16, name="w_grouped", align_bytes=64)
+            nc.gpsimd.tensor_scalar(
+                out=grouped[:],
+                in0=w_raw[b][:, g].rearrange("p t o -> p o t"),
+                scalar1=1.0,
+                scalar2=0.0,
+                op0=MULT,
+                op1=ADD,
+            )
+            w_grouped[m] = grouped
 
-        def quantise_w(b):
-            codes = w_pool.tile([P, GROUPS * O], U32, name="w_codes", align_bytes=64)
-            scales = w_pool.tile([P, GROUPS * O], U8, name="w_scales", align_bytes=64)
-            quantise(nc, codes[:], scales[:], w_grouped[b][:])
-            w_mx[b] = (codes, scales)
+        def quantise_w(m):
+            b, g = divmod(m, GROUPS)
+            if g == 0:
+                codes = w_pool.tile([P, GROUPS * O], U32, name="w_codes", align_bytes=64)
+                scales = w_pool.tile([P, GROUPS * O], U8, name="w_scales", align_bytes=64)
+                w_mx[b] = (codes, scales)
+            codes, scales = w_mx[b]
+            cols = slice(g * O, (g + 1) * O)
+            quantise(nc, codes[:, cols], scales[:, cols], w_grouped[m][:])
 
         def output(n, lo=0, hi=UNIT):
             w_codes, w_scales = w_mx[n // UNITS_PER_DATASET]
@@ -300,12 +308,15 @@ def tile_mlpmodelpredictor_pb_t_kernel(tc, z2, sw1, b2, w3, b3, out):
         quantise_h(0, 0)
         load_z(4)
         load_w(1)
-        regroup_w(0, nc.vector.tensor_copy)
+        for g in range(GROUPS):
+            w_grouped[g] = keep.tile([P, O, PACK], BF16, name="w_first%d" % g, align_bytes=64)
+            regroup(nc.vector.tensor_copy, w_grouped[g][:], w_raw[0][:, g])
         transpose_z(2, 0)
         transpose_z(2, 1)
         copy_z(2, 0, nc.scalar.copy)
         copy_z(2, 1, nc.scalar.copy)
         quantise_w(0)
+        quantise_w(1)
 
         last = UNITS - 1
         for n in range(1, last):
@@ -325,16 +336,16 @@ def tile_mlpmodelpredictor_pb_t_kernel(tc, z2, sw1, b2, w3, b3, out):
                 transpose_z(n + 2, 0)
                 transpose_z(n + 2, 1)
                 copy_z(n + 2, 0, nc.scalar.copy)
-                copy_z(n + 2, 1, nc.scalar.copy if new_dataset else nc.vector.tensor_copy)
             for lo, hi in HALVES if n + 1 == last else [(0, UNIT)]:
                 hidden(n, 1, lo, hi)
             regroup_h(n, 0)
-            if new_dataset:
-                regroup_w(b, nc.vector.tensor_copy)
+            if n >= 2:
+                quantise_w(n)
+            regroup_w(n + 1)
+            if n + 2 < UNITS:
+                copy_z(n + 2, 1, nc.vector.tensor_copy)
             if n >= 2:
                 store(n - 2)
-            if new_dataset:
-                quantise_w(b)
             quantise_h(n, 0)
 
         output(last - 2)
@@ -343,13 +354,15 @@ def tile_mlpmodelpredictor_pb_t_kernel(tc, z2, sw1, b2, w3, b3, out):
             regroup_h(last - 1, 1, lo, hi)
         for lo, hi in HALVES:
             quantise_h(last - 1, 1, lo, hi)
-        before = (last - 1, 0, UNIT)
+        quantise_w(last)
         for lo, hi in LAST_PIECES:
             for g in range(GROUPS):
                 hidden(last, g, lo, hi)
+        before = (last - 1, 0, UNIT)
+        for lo, hi in LAST_PIECES:
             output(*before)
             for g in range(GROUPS):
-                regroup_h(last, g, lo, hi)
+                regroup_h(last, g, lo, hi, nc.scalar.copy if hi == UNIT else nc.vector.tensor_copy)
             store(*before)
             for g in range(GROUPS):
                 quantise_h(last, g, lo, hi)

@@ -32,8 +32,8 @@ FLOPS = 2 * T * B * R * H + 2 * T * B * H * O
 
 def regroup(copy, grouped, planes):
     copy(
-        out=grouped.rearrange("p (c i) t -> p c t i", i=4),
-        in_=planes.rearrange("p t (c i) -> p c t i", i=4),
+        out=grouped.rearrange("p (c i) t -> p c t i", i=8),
+        in_=planes.rearrange("p t (c i) -> p c t i", i=8),
     )
 
 

@@ -229,6 +229,17 @@ def tile_mlpmodelpredictor_pb_t_kernel(tc, z2, sw1, b2, w3, b3, out):
         s_rows = keep.tile([P, 2, PACK, UNIT], BF16, name="s_rows")
         b2_rows = keep.tile([P, P * PACK], BF16, name="b2_rows")
         b3_all = keep.tile([P, B, O], BF16, name="b3_all")
+        zeros = keep.tile([P, UNIT], BF16, name="zeros")
+        nc.vector.memset(zeros[:], 0.0)
+        idle_bank = psum_u.tile([P, UNIT], F32, name="u_bank")
+
+        def keep_warm(passes):
+            for i in range(passes):
+                nc.tensor.matmul(
+                    out=idle_bank[:], lhsT=zeros[:, 0:P], rhs=zeros[:], start=True, stop=True
+                )
+
+        keep_warm(5)
         nc.vector.memset(b2_rows[:], 0.0)
         load_z(0, 0, HALF)
         nc.sync.dma_start(
@@ -278,6 +289,7 @@ def tile_mlpmodelpredictor_pb_t_kernel(tc, z2, sw1, b2, w3, b3, out):
         for t in range(PACK):
             nc.tensor.transpose(out=b2_bank[:, t, :], in_=b2_rows_f32[:, t, :], identity=ident[:])
         transpose_z(0, 1)
+        keep_warm(1)
         regroup_s(0, 0, nc.vector.tensor_copy)
         regroup_s(0, 1, nc.scalar.copy)
         quantise_z(0, 0, HALF)
@@ -355,12 +367,15 @@ def tile_mlpmodelpredictor_pb_t_kernel(tc, z2, sw1, b2, w3, b3, out):
         for lo, hi in HALVES:
             quantise_h(last - 1, 1, lo, hi)
         quantise_w(last)
-        for lo, hi in LAST_PIECES:
+        before = (last - 1, 0, UNIT)
+        for i, (lo, hi) in enumerate(LAST_PIECES):
+            if i == 2:
+                output(*before)
             for g in range(GROUPS):
                 hidden(last, g, lo, hi)
-        before = (last - 1, 0, UNIT)
         for lo, hi in LAST_PIECES:
-            output(*before)
+            if lo > 0:
+                output(*before)
             for g in range(GROUPS):
                 regroup_h(last, g, lo, hi, nc.scalar.copy if hi == UNIT else nc.vector.tensor_copy)
             store(*before)

@@ -55,7 +55,7 @@ def tile_mlpmodelpredictor_pb_t_kernel(tc, z2, sw1, b2, w3, b3, out):
         plane_pool = stack.enter_context(tc.tile_pool(name="planes", bufs=4))
         h_pool = stack.enter_context(tc.tile_pool(name="h", bufs=2))
         h_mx_pool = stack.enter_context(tc.tile_pool(name="h_mx", bufs=3 * GROUPS))
-        out_pool = stack.enter_context(tc.tile_pool(name="out", bufs=3))
+        out_pool = stack.enter_context(tc.tile_pool(name="out", bufs=6))
         psum_z = stack.enter_context(tc.psum_pool(name="psum_z", bufs=1))
         psum_u = stack.enter_context(tc.psum_pool(name="psum_u", bufs=4))
         psum_o = stack.enter_context(tc.psum_pool(name="psum_o", bufs=2))
@@ -229,17 +229,17 @@ def tile_mlpmodelpredictor_pb_t_kernel(tc, z2, sw1, b2, w3, b3, out):
         s_rows = keep.tile([P, 2, PACK, UNIT], BF16, name="s_rows")
         b2_rows = keep.tile([P, P * PACK], BF16, name="b2_rows")
         b3_all = keep.tile([P, B, O], BF16, name="b3_all")
-        zeros = keep.tile([P, UNIT], BF16, name="zeros")
+        zeros = keep.tile([P, HALF], BF16, name="zeros")
         nc.vector.memset(zeros[:], 0.0)
         idle_bank = psum_u.tile([P, UNIT], F32, name="u_bank")
 
         def keep_warm(passes):
             for i in range(passes):
                 nc.tensor.matmul(
-                    out=idle_bank[:], lhsT=zeros[:, 0:P], rhs=zeros[:], start=True, stop=True
+                    out=idle_bank[:, 0:HALF], lhsT=zeros[:, 0:P], rhs=zeros[:], start=True, stop=True
                 )
 
-        keep_warm(5)
+        keep_warm(10)
         nc.vector.memset(b2_rows[:], 0.0)
         load_z(0, 0, HALF)
         nc.sync.dma_start(
@@ -289,7 +289,7 @@ def tile_mlpmodelpredictor_pb_t_kernel(tc, z2, sw1, b2, w3, b3, out):
         for t in range(PACK):
             nc.tensor.transpose(out=b2_bank[:, t, :], in_=b2_rows_f32[:, t, :], identity=ident[:])
         transpose_z(0, 1)
-        keep_warm(1)
+        keep_warm(2)
         regroup_s(0, 0, nc.vector.tensor_copy)
         regroup_s(0, 1, nc.scalar.copy)
         quantise_z(0, 0, HALF)
@@ -326,7 +326,7 @@ def tile_mlpmodelpredictor_pb_t_kernel(tc, z2, sw1, b2, w3, b3, out):
         transpose_z(2, 0)
         transpose_z(2, 1)
         copy_z(2, 0, nc.scalar.copy)
-        copy_z(2, 1, nc.scalar.copy)
+        copy_z(2, 1, nc.vector.tensor_copy)
         quantise_w(0)
         quantise_w(1)
 
@@ -354,10 +354,10 @@ def tile_mlpmodelpredictor_pb_t_kernel(tc, z2, sw1, b2, w3, b3, out):
             if n >= 2:
                 quantise_w(n)
             regroup_w(n + 1)
-            if n + 2 < UNITS:
-                copy_z(n + 2, 1, nc.vector.tensor_copy)
             if n >= 2:
                 store(n - 2)
+            if n + 2 < UNITS:
+                copy_z(n + 2, 1, nc.vector.tensor_copy)
             quantise_h(n, 0)
 
         output(last - 2)

@@ -11,6 +11,7 @@ FP8X4 = mybir.dt.float8_e4m3fn_x4
 RELU = mybir.ActivationFunctionType.Relu
 ADD = mybir.AluOpType.add
 MULT = mybir.AluOpType.mult
+MAX = mybir.AluOpType.max
 
 T, B, R, H, O = 1024, 8, 512, 1024, 128
 P = 128
@@ -71,6 +72,7 @@ def tile_mlpmodelpredictor_pb_t_kernel(tc, z2, sw1, b2, w3, b3, out):
         w_raw = {}
         w_grouped = {}
         w_mx = {}
+        v_banks = {}
         o_banks = {}
 
         def load_z(n, lo=0, hi=UNIT):
@@ -125,11 +127,8 @@ def tile_mlpmodelpredictor_pb_t_kernel(tc, z2, sw1, b2, w3, b3, out):
             codes, scales = z_mx[n]
             quantise(nc, codes[:, lo:hi], scales[:, lo:hi], z_grouped[n][:, lo:hi])
 
-        def hidden_chunk(n, g, t, lo=0, hi=UNIT):
-            b = n // UNITS_PER_DATASET
+        def first_layer(n, g, t, lo=0, hi=UNIT):
             z_codes, z_scales = z_mx[n]
-            if lo == 0 and t == 0:
-                planes[n, g] = plane_pool.tile([P, PACK, UNIT], BF16, name="planes")
             c = g * PACK + t
             cols = slice(c * P, (c + 1) * P)
             u_bank = psum_u.tile([P, UNIT], F32, name="u_bank")
@@ -142,12 +141,38 @@ def tile_mlpmodelpredictor_pb_t_kernel(tc, z2, sw1, b2, w3, b3, out):
                 start=True,
                 stop=True,
             )
+            return u_bank
+
+        def bias_of(n, g, t):
+            c = n // UNITS_PER_DATASET * GROUPS + g
+            return b2_cols[:, t, c : c + 1]
+
+        def hidden_chunk(n, g, t, lo=0, hi=UNIT):
+            if lo == 0 and t == 0:
+                planes[n, g] = plane_pool.tile([P, PACK, UNIT], BF16, name="planes")
+            u_bank = first_layer(n, g, t, lo, hi)
             nc.scalar.activation(
                 out=planes[n, g][:, t, lo:hi],
                 in_=u_bank[:, 0 : hi - lo],
                 func=RELU,
-                bias=b2_cols[:, t, b * GROUPS + g : b * GROUPS + g + 1],
+                bias=bias_of(n, g, t),
                 scale=1.0,
+            )
+
+        def hidden_shared(n, g):
+            planes[n, g] = plane_pool.tile([P, PACK, UNIT], BF16, name="planes")
+            v_banks[n, g] = first_layer(n, g, 0)
+            for t in range(1, PACK):
+                hidden_chunk(n, g, t)
+
+        def activate_on_vector(n, g):
+            nc.vector.tensor_scalar(
+                out=planes[n, g][:, 0, :],
+                in0=v_banks[n, g][:],
+                scalar1=bias_of(n, g, 0),
+                scalar2=0.0,
+                op0=ADD,
+                op1=MAX,
             )
 
         def hidden(n, g, lo=0, hi=UNIT):
@@ -348,16 +373,20 @@ def tile_mlpmodelpredictor_pb_t_kernel(tc, z2, sw1, b2, w3, b3, out):
                 transpose_z(n + 2, 0)
                 transpose_z(n + 2, 1)
                 copy_z(n + 2, 0, nc.scalar.copy)
-            for lo, hi in HALVES if n + 1 == last else [(0, UNIT)]:
-                hidden(n, 1, lo, hi)
+                copy_z(n + 2, 1, nc.scalar.copy)
+            if n + 1 < last:
+                hidden_shared(n, 1)
+            else:
+                for lo, hi in HALVES:
+                    hidden(n, 1, lo, hi)
             regroup_h(n, 0)
             if n >= 2:
                 quantise_w(n)
             regroup_w(n + 1)
+            if n + 1 < last:
+                activate_on_vector(n, 1)
             if n >= 2:
                 store(n - 2)
-            if n + 2 < UNITS:
-                copy_z(n + 2, 1, nc.vector.tensor_copy)
             quantise_h(n, 0)
 
         output(last - 2)

from contextlib import ExitStack

import concourse.mybir as mybir
from concourse.masks import make_identity

F32 = mybir.dt.float32
BF16 = mybir.dt.bfloat16
U32 = mybir.dt.uint32
U8 = mybir.dt.uint8
FP8X4 = mybir.dt.float8_e4m3fn_x4
RELU = mybir.ActivationFunctionType.Relu
ADD = mybir.AluOpType.add
MULT = mybir.AluOpType.mult
MAX = mybir.AluOpType.max

T, B, R, H, O = 1024, 8, 512, 1024, 128
P = 128
PACK = 4
UNIT = 512
UNITS_PER_DATASET = T // UNIT
UNITS = B * UNITS_PER_DATASET
TOKEN_TILES = UNIT // P
CHUNKS = H // P
GROUPS = CHUNKS // PACK
HALF = UNIT // 2
PAIR = 2
AHEAD = 4
HALVES = [(0, HALF), (HALF, UNIT)]
LAST_PIECES = [(0, HALF), (HALF, HALF + P), (HALF + P, UNIT)]

FLOPS = 2 * T * B * R * H + 2 * T * B * H * O


def regroup(copy, grouped, planes):
    copy(
        out=grouped.rearrange("p (c i) t -> p c t i", i=8),
        in_=planes.rearrange("p t (c i) -> p c t i", i=8),
    )


def quantise(nc, codes, scales, grouped):
    nc.vector.quantize_mx(
        out=codes.bitcast(FP8X4),
        scales=scales,
        in_=grouped.rearrange("p c t -> p (c t)"),
    )


def tile_mlpmodelpredictor_pb_t_kernel(tc, z2, sw1, b2, w3, b3, out):
    nc = tc.nc
    with ExitStack() as stack:
        keep = stack.enter_context(tc.tile_pool(name="keep", bufs=1))
        z_raw_pool = stack.enter_context(tc.tile_pool(name="z_raw", bufs=AHEAD))
        w_pool = stack.enter_context(tc.tile_pool(name="w3", bufs=2))
        z_pool = stack.enter_context(tc.tile_pool(name="z", bufs=2))
        plane_pool = stack.enter_context(tc.tile_pool(name="planes", bufs=4))
        h_pool = stack.enter_context(tc.tile_pool(name="h", bufs=2))
        h_mx_pool = stack.enter_context(tc.tile_pool(name="h_mx", bufs=3 * GROUPS))
        out_pool = stack.enter_context(tc.tile_pool(name="out", bufs=6))
        psum_z = stack.enter_context(tc.psum_pool(name="psum_z", bufs=1))
        psum_u = stack.enter_context(tc.psum_pool(name="psum_u", bufs=4))
        psum_o = stack.enter_context(tc.psum_pool(name="psum_o", bufs=2))
        stack.enter_context(tc.manual_schedule())

        z_raw = {}
        z_banks = {}
        z_grouped = {}
        z_mx = {}
        planes = {}
        h_grouped = {}
        h_mx = {}
        w_raw = {}
        w_grouped = {}
        w_mx = {}
        v_banks = {}
        o_banks = {}

        def load_z(n, lo=0, hi=UNIT):
            b, s = divmod(n, UNITS_PER_DATASET)
            if lo == 0:
                z_raw[n] = z_raw_pool.tile([P, TOKEN_TILES, R], BF16, name="z_rows")
            nc.sync.dma_start(
                out=z_raw[n][:, lo // P : hi // P, :],
                in_=z2[s * UNIT + lo : s * UNIT + hi, b, :].rearrange("(j p) r -> p j r", p=P),
            )

        def load_s(col_half):
            nc.sync.dma_start(
                out=s_rows[:, col_half],
                in_=sw1[:, col_half * UNIT : (col_half + 1) * UNIT].rearrange(
                    "(p j) c -> p j c", j=PACK
                ),
            )

        def load_w(b):
            rows = w_pool.tile([P, GROUPS, PACK, O], BF16, name="w_rows")
            nc.sync.dma_start(
                out=rows[:], in_=w3[b].rearrange("(g p t) o -> p g t o", g=GROUPS, t=PACK)
            )
            w_raw[b] = rows

        def transpose_z(n, half):
            words = z_raw[n][:].bitcast(F32)
            bank = psum_z.tile([P, PAIR, HALF], F32, name="z_bank%d" % half)
            for i in range(HALF // P):
                for u in range(PAIR):
                    nc.tensor.transpose(
                        out=bank[:, u, i * P : (i + 1) * P],
                        in_=words[:, half * (HALF // P) + i, u : PAIR * P : PAIR],
                        identity=ident[:],
                    )
            z_banks[n, half] = bank

        def copy_z(n, half, copy):
            if half == 0:
                z_grouped[n] = z_pool.tile([P, UNIT, PACK], BF16, name="z_grouped", align_bytes=64)
            copy(
                out=z_grouped[n][:].bitcast(F32)[:, half * HALF : (half + 1) * HALF, :],
                in_=z_banks[n, half][:].rearrange("p u r -> p r u"),
            )

        def quantise_z(n, lo=0, hi=UNIT):
            if lo == 0:
                codes = z_pool.tile([P, UNIT], U32, name="z_codes", align_bytes=64)
                scales = z_pool.tile([P, UNIT], U8, name="z_scales", align_bytes=64)
                z_mx[n] = (codes, scales)
            codes, scales = z_mx[n]
            quantise(nc, codes[:, lo:hi], scales[:, lo:hi], z_grouped[n][:, lo:hi])

        def first_layer(n, g, t, lo=0, hi=UNIT):
            z_codes, z_scales = z_mx[n]
            c = g * PACK + t
            cols = slice(c * P, (c + 1) * P)
            u_bank = psum_u.tile([P, UNIT], F32, name="u_bank")
            nc.tensor.matmul_mx(
                out=u_bank[:, 0 : hi - lo],
                lhsT=s_codes[:, cols].bitcast(FP8X4),
                lhsT_scale=s_scales[:, cols],
                rhs=z_codes[:, lo:hi].bitcast(FP8X4),
                rhs_scale=z_scales[:, lo:hi],
                start=True,
                stop=True,
            )
            return u_bank

        def bias_of(n, g, t):
            c = n // UNITS_PER_DATASET * GROUPS + g
            return b2_cols[:, t, c : c + 1]

        def hidden_chunk(n, g, t, lo=0, hi=UNIT):
            if lo == 0 and t == 0:
                planes[n, g] = plane_pool.tile([P, PACK, UNIT], BF16, name="planes")
            u_bank = first_layer(n, g, t, lo, hi)
            nc.scalar.activation(
                out=planes[n, g][:, t, lo:hi],
                in_=u_bank[:, 0 : hi - lo],
                func=RELU,
                bias=bias_of(n, g, t),
                scale=1.0,
            )

        def hidden_shared(n, g):
            planes[n, g] = plane_pool.tile([P, PACK, UNIT], BF16, name="planes")
            v_banks[n, g] = first_layer(n, g, 0)
            for t in range(1, PACK):
                hidden_chunk(n, g, t)

        def activate_on_vector(n, g):
            nc.vector.tensor_scalar(
                out=planes[n, g][:, 0, :],
                in0=v_banks[n, g][:],
                scalar1=bias_of(n, g, 0),
                scalar2=0.0,
                op0=ADD,
                op1=MAX,
            )

        def hidden(n, g, lo=0, hi=UNIT):
            for t in range(PACK):
                hidden_chunk(n, g, t, lo, hi)

        def regroup_h(n, g, lo=0, hi=UNIT, copy=nc.vector.tensor_copy):
            if lo == 0:
                h_grouped[n, g] = h_pool.tile(
                    [P, UNIT, PACK], BF16, name="h_grouped", align_bytes=64
                )
            regroup(copy, h_grouped[n, g][:, lo:hi], planes[n, g][:, :, lo:hi])

        def quantise_h(n, g, lo=0, hi=UNIT):
            if lo == 0:
                codes = h_mx_pool.tile([P, UNIT], U32, name="h_codes", align_bytes=64)
                scales = h_mx_pool.tile([P, UNIT], U8, name="h_scales", align_bytes=64)
                h_mx[n, g] = (codes, scales)
            codes, scales = h_mx[n, g]
            quantise(nc, codes[:, lo:hi], scales[:, lo:hi], h_grouped[n, g][:, lo:hi])

        def regroup_w(m):
            b, g = divmod(m, GROUPS)
            grouped = keep.tile([P, O, PACK], BF16, name="w_grouped", align_bytes=64)
            nc.gpsimd.tensor_scalar(
                out=grouped[:],
                in0=w_raw[b][:, g].rearrange("p t o -> p o t"),
                scalar1=1.0,
                scalar2=0.0,
                op0=MULT,
                op1=ADD,
            )
            w_grouped[m] = grouped

        def quantise_w(m):
            b, g = divmod(m, GROUPS)
            if g == 0:
                codes = w_pool.tile([P, GROUPS * O], U32, name="w_codes", align_bytes=64)
                scales = w_pool.tile([P, GROUPS * O], U8, name="w_scales", align_bytes=64)
                w_mx[b] = (codes, scales)
            codes, scales = w_mx[b]
            cols = slice(g * O, (g + 1) * O)
            quantise(nc, codes[:, cols], scales[:, cols], w_grouped[m][:])

        def output(n, lo=0, hi=UNIT):
            w_codes, w_scales = w_mx[n // UNITS_PER_DATASET]
            o_bank = psum_o.tile([P, TOKEN_TILES, O], F32, name="o_bank")
            for j in range(lo // P, hi // P):
                tokens = slice(j * P, (j + 1) * P)
                for g in range(GROUPS):
                    h_codes, h_scales = h_mx[n, g]
                    w_cols = slice(g * O, (g + 1) * O)
                    nc.tensor.matmul_mx(
                        out=o_bank[:, j, :],
                        lhsT=h_codes[:, tokens].bitcast(FP8X4),
                        lhsT_scale=h_scales[:, tokens],
                        rhs=w_codes[:, w_cols].bitcast(FP8X4),
                        rhs_scale=w_scales[:, w_cols],
                        start=(g == 0),
                        stop=(g == GROUPS - 1),
                    )
            o_banks[n, lo] = o_bank

        def store(n, lo=0, hi=UNIT):
            b, s = divmod(n, UNITS_PER_DATASET)
            tiles = slice(lo // P, hi // P)
            result = out_pool.tile([P, TOKEN_TILES, O], F32, name="result")
            nc.vector.tensor_tensor(
                out=result[:, tiles, :],
                in0=o_banks[n, lo][:, tiles, :],
                in1=b3_all[:, b, :].unsqueeze(1).to_broadcast([P, (hi - lo) // P, O]),
                op=ADD,
            )
            nc.sync.dma_start(
                out=out[s * UNIT + lo : s * UNIT + hi, b, :].rearrange("(j p) o -> p j o", p=P),
                in_=result[:, tiles, :],
            )

        s_rows = keep.tile([P, 2, PACK, UNIT], BF16, name="s_rows")
        b2_rows = keep.tile([P, P * PACK], BF16, name="b2_rows")
        b3_all = keep.tile([P, B, O], BF16, name="b3_all")
        zeros = keep.tile([P, HALF], BF16, name="zeros")
        nc.vector.memset(zeros[:], 0.0)
        idle_bank = psum_u.tile([P, UNIT], F32, name="u_bank")

        def keep_warm(passes):
            for i in range(passes):
                nc.tensor.matmul(
                    out=idle_bank[:, 0:HALF], lhsT=zeros[:, 0:P], rhs=zeros[:], start=True, stop=True
                )

        keep_warm(10)
        nc.vector.memset(b2_rows[:], 0.0)
        load_z(0, 0, HALF)
        nc.sync.dma_start(
            out=b2_rows[0 : B * GROUPS, :], in_=b2.rearrange("b (g c) -> (b g) c", g=GROUPS)
        )
        load_s(0)
        load_z(0, HALF, UNIT)
        load_s(1)
        load_z(1)
        load_z(2)
        load_w(0)
        load_z(3)
        nc.sync.dma_start(
            out=b3_all[:].rearrange("p b o -> p (b o)"),
            in_=b3.rearrange("b o -> (b o)").partition_broadcast(P),
        )

        ident = keep.tile([P, P], F32, name="ident")
        make_identity(nc, ident[:])

        b2_rows_f32 = keep.tile([P, PACK, P], F32, name="b2_rows_f32")
        b2_cols = keep.tile([P, PACK, B * GROUPS], F32, name="b2_cols")
        s_grouped = keep.tile([P, 2, UNIT, PACK], BF16, name="s_grouped", align_bytes=64)
        s_codes = keep.tile([P, H], U32, name="s_codes", align_bytes=64)
        s_scales = keep.tile([P, H], U8, name="s_scales", align_bytes=64)

        def regroup_s(col_half, t, copy):
            copy(
                out=s_grouped[:, col_half, t * P : (t + 1) * P, :].rearrange(
                    "p (m i) j -> p m j i", i=2
                ),
                in_=s_rows[:, col_half].rearrange("p j (m i t) -> p t m j i", i=2, t=PACK)[:, t],
            )

        def quantise_s(col_half, t0, t1):
            cols = slice(col_half * UNIT + t0 * P, col_half * UNIT + t1 * P)
            quantise(
                nc, s_codes[:, cols], s_scales[:, cols], s_grouped[:, col_half, t0 * P : t1 * P]
            )

        transpose_z(0, 0)
        copy_z(0, 0, nc.scalar.copy)
        nc.vector.tensor_copy(
            out=b2_rows_f32[:], in_=b2_rows[:].rearrange("q (p t) -> q t p", t=PACK)
        )
        b2_bank = psum_o.tile([P, TOKEN_TILES, O], F32, name="o_bank")
        for t in range(PACK):
            nc.tensor.transpose(out=b2_bank[:, t, :], in_=b2_rows_f32[:, t, :], identity=ident[:])
        transpose_z(0, 1)
        keep_warm(2)
        regroup_s(0, 0, nc.vector.tensor_copy)
        regroup_s(0, 1, nc.scalar.copy)
        quantise_z(0, 0, HALF)
        quantise_s(0, 0, 1)
        nc.vector.tensor_copy(out=b2_cols[:], in_=b2_bank[:, :, 0 : B * GROUPS])
        copy_z(0, 1, nc.scalar.copy)
        hidden_chunk(0, 0, 0, 0, HALF)
        regroup_s(0, 2, nc.vector.tensor_copy)
        quantise_s(0, 1, 2)
        hidden_chunk(0, 0, 1, 0, HALF)
        regroup_s(0, 3, nc.vector.tensor_copy)
        quantise_s(0, 2, 3)
        hidden_chunk(0, 0, 2, 0, HALF)
        quantise_s(0, 3, 4)
        hidden_chunk(0, 0, 3, 0, HALF)
        quantise_z(0, HALF, UNIT)
        hidden(0, 0, HALF, UNIT)
        transpose_z(1, 0)
        transpose_z(1, 1)
        for t in range(PACK):
            regroup_s(1, t, nc.vector.tensor_copy)
        quantise_s(1, 0, PACK)
        copy_z(1, 0, nc.scalar.copy)
        copy_z(1, 1, nc.scalar.copy)
        hidden(0, 1)
        regroup_h(0, 0)
        quantise_z(1)
        quantise_h(0, 0)
        load_z(4)
        load_w(1)
        for g in range(GROUPS):
            w_grouped[g] = keep.tile([P, O, PACK], BF16, name="w_first%d" % g, align_bytes=64)
            regroup(nc.vector.tensor_copy, w_grouped[g][:], w_raw[0][:, g])
        transpose_z(2, 0)
        transpose_z(2, 1)
        copy_z(2, 0, nc.scalar.copy)
        copy_z(2, 1, nc.vector.tensor_copy)
        quantise_w(0)
        quantise_w(1)

        last = UNITS - 1
        for n in range(1, last):
            b = n // UNITS_PER_DATASET
            new_dataset = n % UNITS_PER_DATASET == 0
            if n + AHEAD < UNITS:
                load_z(n + AHEAD)
            if new_dataset and b + 1 < B:
                load_w(b + 1)
            regroup_h(n - 1, 1)
            quantise_z(n + 1)
            hidden(n, 0)
            if n >= 2:
                output(n - 2)
            quantise_h(n - 1, 1)
            if n + 2 < UNITS:
                transpose_z(n + 2, 0)
                transpose_z(n + 2, 1)
                copy_z(n + 2, 0, nc.scalar.copy)
                copy_z(n + 2, 1, nc.scalar.copy)
            if n + 1 < last:
                hidden_shared(n, 1)
            else:
                for lo, hi in HALVES:
                    hidden(n, 1, lo, hi)
            regroup_h(n, 0)
            if n >= 2:
                quantise_w(n)
            regroup_w(n + 1)
            if n + 1 < last:
                activate_on_vector(n, 1)
            if n >= 2:
                store(n - 2)
            quantise_h(n, 0)

        output(last - 2)
        store(last - 2)
        for lo, hi in HALVES:
            regroup_h(last - 1, 1, lo, hi)
        for lo, hi in HALVES:
            quantise_h(last - 1, 1, lo, hi)
        quantise_w(last)
        before = (last - 1, 0, UNIT)
        for i, (lo, hi) in enumerate(LAST_PIECES):
            if i == 2:
                output(*before)
            for g in range(GROUPS):
                hidden(last, g, lo, hi)
        for lo, hi in LAST_PIECES:
            if lo > 0:
                output(*before)
            for g in range(GROUPS):
                regroup_h(last, g, lo, hi, nc.scalar.copy if hi == UNIT else nc.vector.tensor_copy)
            store(*before)
            for g in range(GROUPS):
                quantise_h(last, g, lo, hi)
            before = (last, lo, hi)
        output(*before)
        store(*before)
